import numpy as np
import ml_dtypes


def mxq(x, axis, fmt="e4m3"):
    dtype, down = {"e4m3": (ml_dtypes.float8_e4m3fn, 7), "e5m2": (ml_dtypes.float8_e5m2, 14)}[fmt]
    v = np.moveaxis(np.asarray(x, np.float32).astype(ml_dtypes.bfloat16).astype(np.float64), axis, -1)
    blocks = v.reshape(v.shape[:-1] + (-1, 32))
    amax = np.abs(blocks).max(-1, keepdims=True)
    byte = np.maximum(np.where(amax > 0, np.frexp(amax)[1] - 1 + 127, 0) - down, 1)
    scale = np.exp2(byte - 127.0)
    codes = (blocks / scale).astype(np.float32).astype(dtype).astype(np.float64)
    return np.moveaxis((codes * scale).reshape(v.shape), -1, axis)


WIDE = False


def mx_kscale(k):
    if not WIDE:
        return np.ones(k)
    levels = np.array([10, -10, 5, -5, 0])
    if k % 512:
        return np.exp2(np.random.permutation(np.resize(levels, k // 32))).repeat(32)
    a = np.empty((k // 512, 16))
    for p in range(k // 512):
        a[p, :8] = np.random.permutation(np.resize(levels, 8))
        for g in range(8):
            far = levels[np.abs(levels - a[p, g]) >= 10]
            a[p, g + 8] = far[np.random.randint(len(far))]
    return np.exp2(a.ravel()).repeat(32)


BF16 = ml_dtypes.bfloat16


def bf(x):
    return np.asarray(x, np.float32).astype(BF16)


def f64(x):
    return np.asarray(x).astype(np.float64)


B, D, S, O = 1024, 512, 1024, 256
K1 = D + S
P = S // 2
EPS = 1e-6


def sigmoid(v):
    return 1.0 / (1.0 + np.exp(-v))


def draw0():
    r = np.random.standard_normal
    s = np.concatenate([mx_kscale(D), np.ones(S)])
    t = mx_kscale(S)
    return {
        "inputs": bf(r((B, D)) * s[:D]),
        "states": bf(r((B, S))),
        "W1": bf(r((K1, S)) / np.sqrt(K1) / s[:, None] * t),
        "b1": bf(r(S) * 0.2 * t),
        "W2": bf(r((S, P)) / np.sqrt(S) / t[:, None]),
        "b2": bf(r(P) * 0.2),
        "excitatory_potential": bf(1.0 + 0.1 * r(S)),
        "inhibitory_potential": bf(-1.0 + 0.1 * r(S)),
        "capacitance": bf(1.0 + 0.1 * r(S)),
        "max_conductance": bf(1.0 + 0.1 * r((S, 2))),
        "mean_conductance_potential": bf(0.3 * r((S, 2))),
        "std_conductance": bf(1.0 + 0.2 * r((S, 2))),
        "gamma": bf(1.0 + 0.1 * r(S)),
        "beta": bf(0.1 * r(S)),
    }


def core(inputs, states, W1, b1, W2, b2, excitatory_potential, inhibitory_potential, capacitance,
              max_conductance, mean_conductance_potential, std_conductance, gamma, beta):
    v = f64(states)
    b, s = v.shape
    intervals = np.ones((b, 1))
    cat = np.concatenate([f64(inputs), v], -1)
    h = (mxq(cat, 1, "e4m3") @ mxq(f64(W1), 0, "e4m3")) + f64(b1)
    pre = (mxq(h, 1, "e4m3") @ mxq(f64(W2), 0, "e4m3")) + f64(b2)
    memory_cell_inputs = np.stack([pre, -pre], -1).reshape(b, s)
    pairs = v.reshape(b, s // 2, 2)
    rolled = np.roll(pairs, 1, axis=-1)
    presyn = np.concatenate([pairs, rolled], -1).reshape(b, s, 2)
    g = f64(max_conductance) * sigmoid(f64(std_conductance) * (presyn - f64(mean_conductance_potential)))
    rev = np.stack([f64(excitatory_potential), f64(inhibitory_potential)], -1)
    diff = rev - v[..., None]
    states_change = (memory_cell_inputs + np.sum(g * diff, -1)) / f64(capacitance) * intervals
    x = v + states_change
    mu = np.mean(x, -1, keepdims=True)
    var = np.mean((x - mu) ** 2, -1, keepdims=True)
    return (x - mu) * (1.0 / np.sqrt(var + EPS)) * f64(gamma) + f64(beta)


def e4m3fn_bytes(y):
    return np.clip(np.asarray(y, np.float64), -448.0, 448.0).astype(np.float32).astype(ml_dtypes.float8_e4m3fn).view(np.uint8)


def e4m3fn_values(b):
    return np.asarray(b, np.uint8).view(ml_dtypes.float8_e4m3fn).astype(np.float64)


def setup_inputs():
    d = draw0()
    x0 = np.asarray(d['inputs']).astype(np.float64)
    s = (np.max(np.abs(x0), axis=(0,), keepdims=True) / 448.0).astype(np.float32)
    out = {}
    for k, v in d.items():
        if k == 'inputs':
            out['inputs_bytes'] = e4m3fn_bytes(x0 / s.astype(np.float64))
            out['inputs_scale'] = s
        else:
            out[k] = v
    return out


def reference(inputs_bytes, inputs_scale, states, W1, b1, W2, b2, excitatory_potential, inhibitory_potential, capacitance, max_conductance, mean_conductance_potential, std_conductance, gamma, beta):
    return core(e4m3fn_values(inputs_bytes) * inputs_scale.astype(np.float64), states, W1, b1, W2, b2, excitatory_potential, inhibitory_potential, capacitance, max_conductance, mean_conductance_potential, std_conductance, gamma, beta)

from contextlib import ExitStack

import concourse.mybir as mybir
from concourse.masks import make_identity

B, D, S, O = 1024, 512, 1024, 512
FLOPS = 2 * B * (D + S) * S + 2 * B * S * O

F32 = mybir.dt.float32
BF16 = mybir.dt.bfloat16
U32 = mybir.dt.uint32
U8 = mybir.dt.uint8
FP8 = mybir.dt.float8_e4m3fn
FP8X4 = mybir.dt.float8_e4m3fn_x4
ACT = mybir.ActivationFunctionType
ALU = mybir.AluOpType

P = 128
NT = B // P
EPS = 1e-6

W1_ON_V = ((1, 0),(1,1),(2,0))
BN_ON_S = (3,5,6,7)
W2_ON_V = ()
TS1_ON_V = ()


def tile_memorylayercell_pa_kernel(
    tc, inputs_bytes, inputs_scale, states, W1, b1, W2, b2, excitatory, inhibitory,
    capacitance, max_conductance, mean_conductance, std_conductance, gamma, beta, out,
):
    nc = tc.nc
    with ExitStack() as ctx:
        keep = ctx.enter_context(tc.tile_pool(name="keep", bufs=1))
        wraw_pool = ctx.enter_context(tc.tile_pool(name="wraw", bufs=3))
        wgrp_pool = ctx.enter_context(tc.tile_pool(name="wgrp", bufs=3))
        wide_pool = ctx.enter_context(tc.tile_pool(name="wide", bufs=4))
        igrp_pool = ctx.enter_context(tc.tile_pool(name="igrp", bufs=2))
        cell_pool = ctx.enter_context(tc.tile_pool(name="cell", bufs=2))
        hb_pool = ctx.enter_context(tc.tile_pool(name="hb", bufs=3))
        mem_pool = ctx.enter_context(tc.tile_pool(name="mem", bufs=2))
        ln_pool = ctx.enter_context(tc.tile_pool(name="ln", bufs=2))
        front = ctx.enter_context(tc.psum_pool(name="front", bufs=3))
        prep = ctx.enter_context(tc.psum_pool(name="prep", bufs=2))
        xp = ctx.enter_context(tc.psum_pool(name="xp", bufs=3))

        warm = keep.tile([P, 1], F32, name="warm")
        nc.vector.memset(warm[:], 0.0)
        warm2 = keep.tile([P, 1], F32, name="warm2")
        nc.scalar.activation(out=warm2[:], in_=warm[:], func=ACT.Sigmoid)

        ident = keep.tile([P, P], F32, name="ident")
        make_identity(nc, ident[:])

        st_view = states.rearrange("(p i) d -> p i d", i=NT)
        out_view = out.rearrange("(p i) d -> p i d", i=NT)
        st_raw = []
        for k in range(4):
            t = keep.tile([P, 2, S], BF16, name=f"st_raw{k}")
            st_raw.append(t)
        w1_view = W1.rearrange("(c p j) n -> c p j n", p=P, j=4)
        w1_raw = []
        for c in range(3):
            t = wraw_pool.tile([P, 4, S], BF16, name="w_raw")
            w1_raw.append(t)
        by = keep.tile([P, NT, D], U8, name="in_bytes")
        scale_bc = keep.tile([P, D], F32, name="scale_bc")

        def load_col(v, name):
            t = keep.tile([P, 2, 4], BF16, name=name)
            nc.scalar.dma_start(out=t[:], in_=v.rearrange("(g p t) -> p g t", g=2, t=4))
            return t

        def load_col2(v, name):
            t = keep.tile([P, 2, 4, 2], BF16, name=name)
            nc.scalar.dma_start(out=t[:], in_=v.rearrange("(g p t) s -> p g t s", g=2, t=4))
            return t

        sd_b = load_col2(std_conductance, "sd_b")
        mn_b = load_col2(mean_conductance, "mn_b")
        cap_b = load_col(capacitance, "cap_b")
        mc_b = load_col2(max_conductance, "mc_b")
        exc_b = load_col(excitatory, "exc_b")
        inh_b = load_col(inhibitory, "inh_b")
        b1_b = load_col(b1, "b1_b")
        b2_b = keep.tile([P, 2, 2], BF16, name="b2_b")
        nc.scalar.dma_start(out=b2_b[:], in_=b2.rearrange("(g p u) -> p g u", g=2, u=2))

        for k in range(2):
            nc.sync.dma_start(out=st_raw[k][:], in_=st_view[:, 2 * k : 2 * k + 2, :])
        for c in (1, 2, 0):
            nc.sync.dma_start(out=w1_raw[c][:], in_=w1_view[c])
        nc.sync.dma_start(out=by[:], in_=inputs_bytes.rearrange("(p i) d -> p i d", i=NT))
        nc.sync.dma_start(out=scale_bc[:], in_=inputs_scale.rearrange("o k -> (o k)").partition_broadcast(P))
        for k in range(2, 4):
            nc.sync.dma_start(out=st_raw[k][:], in_=st_view[:, 2 * k : 2 * k + 2, :])
        w2_both = wraw_pool.tile([P, 2, 4, O], BF16, name="w_raw")
        nc.sync.dma_start(out=w2_both[:], in_=W2.rearrange("(c p j) n -> p c j n", p=P, j=4))
        w2_raw = [w2_both[:, 0], w2_both[:, 1]]
        gam = keep.tile([P, S], BF16, name="gam")
        nc.sync.dma_start(out=gam[:], in_=gamma.partition_broadcast(P))
        bet = keep.tile([P, S], BF16, name="bet")
        nc.sync.dma_start(out=bet[:], in_=beta.partition_broadcast(P))

        sd = keep.tile([P, 2, 4, 2], F32, name="sd")
        nc.vector.tensor_copy(out=sd[:], in_=sd_b[:])
        off = keep.tile([P, 2, 4, 2], F32, name="off")
        nc.vector.scalar_tensor_tensor(out=off[:], in0=mn_b[:], scalar=-1.0, in1=sd_b[:], op0=ALU.mult, op1=ALU.mult)
        rc = keep.tile([P, 2, 4], F32, name="rc")
        nc.vector.reciprocal(out=rc[:], in_=cap_b[:])
        amp = keep.tile([P, 2, 2, 4], F32, name="amp")
        for s in range(2):
            nc.vector.scalar_tensor_tensor(
                out=amp[:, s], in0=mc_b[:, :, :, s], scalar=-1.0, in1=rc[:], op0=ALU.mult, op1=ALU.mult)
        exc = keep.tile([P, 2, 4], F32, name="exc")
        nc.vector.tensor_copy(out=exc[:], in_=exc_b[:])
        inh = keep.tile([P, 2, 4], F32, name="inh")
        nc.vector.tensor_copy(out=inh[:], in_=inh_b[:])
        rcs = keep.tile([P, 4, 2], F32, name="rcs")
        rc_pairs = rc[:].rearrange("p g (u e) -> p (g u) e", e=2)
        nc.vector.tensor_copy(out=rcs[:, :, 0], in_=rc_pairs[:, :, 0])
        nc.vector.tensor_scalar(out=rcs[:, :, 1], in0=rc_pairs[:, :, 1], scalar1=-1.0, scalar2=None, op0=ALU.mult)
        kap = keep.tile([P, 4, 2], F32, name="kap")
        nc.vector.tensor_tensor(
            out=kap[:], in0=rcs[:],
            in1=b2_b[:].rearrange("p g u -> p (g u)").unsqueeze(2).to_broadcast([P, 4, 2]), op=ALU.mult)
        kap2 = keep.tile([P, 4, 2], F32, name="kap2")
        nc.vector.tensor_tensor(out=kap2[:], in0=kap[:], in1=inh[:].rearrange("p g (u e) -> p (g u) e", e=2), op=ALU.add)
        nhalf = keep.tile([P, 1], F32, name="nhalf")
        nc.vector.memset(nhalf[:], -0.5)

        diag = keep.tile([P, 2, 4, P], F32, name="diag")
        nc.gpsimd.tensor_tensor(
            out=diag[:].rearrange("p g t n -> p (g t) n"), in0=ident[:].unsqueeze(1).to_broadcast([P, 8, P]),
            in1=amp[:, 0].rearrange("p g t -> p (g t)").unsqueeze(2).to_broadcast([P, 8, P]), op=ALU.mult)

        vt = []
        for hf in range(2):
            t = keep.tile([P, 4, 2, P, 4], BF16, name=f"vt{hf}", align_bytes=64)
            vt.append(t)
        sq = keep.tile([P, NT, 2, P], U32, name="sq", align_bytes=64)
        ss = keep.tile([P, NT, 2, P], U8, name="ss", align_bytes=64)
        iq = keep.tile([P, NT, P], U32, name="iq", align_bytes=64)
        isc = keep.tile([P, NT, P], U8, name="isc", align_bytes=64)
        w1q = keep.tile([P, 3, S], U32, name="w1q", align_bytes=64)
        w1s = keep.tile([P, 3, S], U8, name="w1s", align_bytes=64)
        w2q = keep.tile([P, 2, O], U32, name="w2q", align_bytes=64)
        w2s = keep.tile([P, 2, O], U8, name="w2s", align_bytes=64)
        hq = keep.tile([P, NT, 2, P], U32, name="hq", align_bytes=64)
        hs = keep.tile([P, NT, 2, P], U8, name="hs", align_bytes=64)

        def states_tile(i):
            hf, ii = i // 4, i % 4
            words = st_raw[i // 2][:, i % 2, :].bitcast(F32)
            bank = front.tile([P, 2, 2, P], F32, name="fbank")
            for g in range(2):
                for u in range(2):
                    nc.tensor.transpose(bank[:, g, u, :], words[:, 256 * g + u : 256 * (g + 1) : 2], ident[:])
            nc.scalar.copy(
                out=vt[hf][:, ii].bitcast(F32), in_=bank[:].rearrange("p g u r -> p g r u"))
            nc.vector.quantize_mx(
                out=sq[:, i].rearrange("p g r -> p (g r)").bitcast(FP8X4),
                scales=ss[:, i].rearrange("p g r -> p (g r)"),
                in_=vt[hf][:, ii].rearrange("p g r t -> p (g r t)"))

        def inputs_pair(k):
            bank = front.tile([P, 2, 2, P], F32, name="fbank")
            for ii in range(2):
                wide = wide_pool.tile([P, D], BF16, name="wide")
                nc.vector.tensor_tensor(out=wide[:], in0=by[:, 2 * k + ii, :].bitcast(FP8), in1=scale_bc[:], op=ALU.mult)
                words = wide[:].bitcast(F32)
                for u in range(2):
                    nc.tensor.transpose(bank[:, ii, u, :], words[:, u : 256 : 2], ident[:])
            grp = igrp_pool.tile([P, 2, P, 4], BF16, name="igrp", align_bytes=64)
            nc.scalar.copy(out=grp[:].bitcast(F32), in_=bank[:].rearrange("p i u r -> p i r u"))
            nc.vector.quantize_mx(
                out=iq[:, 2 * k : 2 * k + 2].rearrange("p i r -> p (i r)").bitcast(FP8X4),
                scales=isc[:, 2 * k : 2 * k + 2].rearrange("p i r -> p (i r)"),
                in_=grp[:].rearrange("p i r t -> p (i r t)"))

        def w1_part(c, g):
            grp = wgrp_pool.tile([P, 512, 4], BF16, name="wgrp", align_bytes=64)
            src = w1_raw[c][:, :, 512 * g : 512 * (g + 1)].rearrange("p j (m t) -> p t m j", t=4)
            dst = grp[:].rearrange("p (t m) j -> p t m j", t=4)
            if (c, g) in W1_ON_V:
                nc.vector.tensor_copy(out=dst, in_=src)
            else:
                nc.scalar.copy(out=dst, in_=src)
            nc.vector.quantize_mx(
                out=w1q[:, c, 512 * g : 512 * (g + 1)].bitcast(FP8X4),
                scales=w1s[:, c, 512 * g : 512 * (g + 1)],
                in_=grp[:].rearrange("p w j -> p (w j)"))

        def w2_part(c):
            grp = wgrp_pool.tile([P, 512, 4], BF16, name="wgrp", align_bytes=64)
            for g in range(2):
                src = w2_raw[c][:, :, 256 * g : 256 * (g + 1)].rearrange("p j (m u) -> p u m j", u=2)
                dst = grp[:, 256 * g : 256 * (g + 1), :].rearrange("p (u m) j -> p u m j", u=2)
                if (c, g) in W2_ON_V:
                    nc.vector.tensor_copy(out=dst, in_=src)
                else:
                    nc.scalar.copy(out=dst, in_=src)
            nc.vector.quantize_mx(
                out=w2q[:, c, :].bitcast(FP8X4), scales=w2s[:, c, :], in_=grp[:].rearrange("p w j -> p (w j)"))

        src_a = [None, None]
        src_b = [None, None]

        def cell_half(hf):
            a_t = cell_pool.tile([P, 8, 512], F32, name="cell_a")
            b_t = cell_pool.tile([P, 8, 512], F32, name="cell_b")
            src_a[hf] = a_t
            src_b[hf] = b_t
            for g in range(2):
                for t in range(4):
                    k = 4 * g + t
                    av = a_t[:, k, :].rearrange("p (i r) -> p i r", i=4)
                    bv = b_t[:, k, :].rearrange("p (i r) -> p i r", i=4)
                    v = vt[hf][:, :, g, :, t]
                    vp = vt[hf][:, :, g, :, t ^ 1]
                    nc.scalar.activation(out=av, in_=v, func=ACT.Sigmoid, bias=off[:, g, t, 0:1], scale=sd[:, g, t, 0:1])
                    nc.scalar.activation(out=bv, in_=vp, func=ACT.Sigmoid, bias=off[:, g, t, 1:2], scale=sd[:, g, t, 1:2])
                    nc.vector.scalar_tensor_tensor(out=av, in0=v, scalar=exc[:, g, t : t + 1], in1=av, op0=ALU.subtract, op1=ALU.mult)
                    if (hf, k) in TS1_ON_V:
                        nc.vector.tensor_scalar(out=b_t[:, k, :], in0=b_t[:, k, :], scalar1=amp[:, 1, g, t : t + 1], scalar2=1.0, op0=ALU.mult, op1=ALU.add)
                    else:
                        nc.scalar.activation(out=b_t[:, k, :], in_=b_t[:, k, :], func=ACT.Identity, bias=1.0, scale=amp[:, 1, g, t : t + 1])
                    nc.vector.scalar_tensor_tensor(out=bv, in0=v, scalar=inh[:, g, t : t + 1], in1=bv, op0=ALU.subtract, op1=ALU.mult)

        def stage1(i):
            hb = hb_pool.tile([P, 2, P, 4], BF16, name="hb", align_bytes=64)
            for g in range(2):
                bank = front.tile([P, 4, P], F32, name="fbank")
                for t in range(4):
                    cols = slice(512 * g + 128 * t, 512 * g + 128 * (t + 1))
                    for n, c in enumerate((1, 2, 0)):
                        rq = iq[:, i] if c == 0 else sq[:, i, c - 1]
                        rs = isc[:, i] if c == 0 else ss[:, i, c - 1]
                        nc.tensor.matmul_mx(
                            out=bank[:, t, :], lhsT=w1q[:, c, cols].bitcast(FP8X4), lhsT_scale=w1s[:, c, cols],
                            rhs=rq.bitcast(FP8X4), rhs_scale=rs, start=(n == 0), stop=(n == 2))
                nc.vector.tensor_tensor(
                    out=hb[:, g], in0=bank[:].rearrange("p t n -> p n t"),
                    in1=b1_b[:, g, :].unsqueeze(1).to_broadcast([P, P, 4]), op=ALU.add)
            nc.vector.quantize_mx(
                out=hq[:, i].rearrange("p g n -> p (g n)").bitcast(FP8X4), scales=hs[:, i].rearrange("p g n -> p (g n)"),
                in_=hb[:].rearrange("p g n t -> p (g n t)"))

        mem = [None] * 4

        def stage2(c2):
            m_t = mem_pool.tile([P, 8, 256], F32, name="mem")
            mem[c2] = m_t
            for g in range(2):
                bank = prep.tile([P, 2, 256], F32, name="pbank")
                for u in range(2):
                    cols = slice(256 * g + 128 * u, 256 * g + 128 * (u + 1))
                    for jj in range(2):
                        for c in range(2):
                            nc.tensor.matmul_mx(
                                out=bank[:, u, P * jj : P * (jj + 1)], lhsT=w2q[:, c, cols].bitcast(FP8X4), lhsT_scale=w2s[:, c, cols],
                                rhs=hq[:, 2 * c2 + jj, c].bitcast(FP8X4), rhs_scale=hs[:, 2 * c2 + jj, c],
                                start=(c == 0), stop=(c == 1))
                for u in range(2):
                    for e in range(2):
                        nc.scalar.activation(
                            out=m_t[:, 4 * g + 2 * u + e, :], in_=bank[:, u, :], func=ACT.Identity,
                            bias=kap2[:, 2 * g + u, e : e + 1], scale=rcs[:, 2 * g + u, e : e + 1])

        def norm(i):
            hf, ii = i // 4, i % 4
            c2, jj = i // 2, i % 2
            stats = ln_pool.tile([P, 2, 6], F32, name="stats")
            banks = []
            for g in range(2):
                bank = xp.tile([P, 4, P], F32, name="xbank")
                banks.append(bank)
                for t in range(4):
                    k = 4 * g + t
                    nc.tensor.matmul(bank[:, t, :], lhsT=src_b[hf][:, k, 128 * ii : 128 * (ii + 1)], rhs=ident[:], is_transpose=True, start=True, stop=False)
                    nc.tensor.matmul(bank[:, t, :], lhsT=src_a[hf][:, k, 128 * ii : 128 * (ii + 1)], rhs=diag[:, g, t, :], start=False, stop=False)
                    nc.tensor.matmul(bank[:, t, :], lhsT=mem[c2][:, k, 128 * jj : 128 * (jj + 1)], rhs=ident[:], is_transpose=True, start=False, stop=True)
                if i not in BN_ON_S:
                    nc.vector.bn_stats(out=stats[:, g, :], in_=bank[:].rearrange("p t n -> p (t n)"))
            w = ln_pool.tile([P, S], F32, name="w")
            mv = ln_pool.tile([P, 2], F32, name="mv")
            ve = ln_pool.tile([P, 1], F32, name="ve")
            sh_op = ALU.subtract
            if i in BN_ON_S:
                sh_op = ALU.add
                sums = ln_pool.tile([P, 2], F32, name="sums")
                sqs = ln_pool.tile([P, 2], F32, name="sqs")
                tot = ln_pool.tile([P, 2], F32, name="tot")
                for g in range(2):
                    nc.scalar.activation(out=w[:, 512 * g : 512 * (g + 1)], in_=banks[g][:].rearrange("p t n -> p (t n)"), func=ACT.Identity, accum_out=sums[:, g : g + 1])
                nc.gpsimd.tensor_tensor(out=tot[:, 0:1], in0=sums[:, 0:1], in1=sums[:, 1:2], op=ALU.add)
                nc.gpsimd.tensor_scalar(out=mv[:, 0:1], in0=tot[:, 0:1], scalar1=-1.0 / S, scalar2=None, op0=ALU.mult)
                for g in range(2):
                    nc.scalar.activation(out=w[:, 512 * g : 512 * (g + 1)], in_=banks[g][:].rearrange("p t n -> p (t n)"), func=ACT.Square, bias=mv[:, 0:1], accum_out=sqs[:, g : g + 1])
                nc.gpsimd.tensor_tensor(out=tot[:, 1:2], in0=sqs[:, 0:1], in1=sqs[:, 1:2], op=ALU.add)
                nc.gpsimd.tensor_scalar(out=ve[:], in0=tot[:, 1:2], scalar1=1.0 / S, scalar2=EPS, op0=ALU.mult, op1=ALU.add)
            else:
                nc.vector.bn_aggr(out=mv[:], in_=stats[:].rearrange("p a b -> p (a b)"))
                nc.gpsimd.tensor_scalar(out=ve[:], in0=mv[:, 1:2], scalar1=EPS, scalar2=None, op0=ALU.add)
            rstd = ln_pool.tile([P, 1], F32, name="rstd")
            nc.gpsimd.tensor_tensor(out=rstd[:], in0=ve[:], in1=nhalf[:], op=ALU.pow)
            for g in range(2):
                nc.vector.scalar_tensor_tensor(
                    out=w[:, 512 * g : 512 * (g + 1)].rearrange("p (n t) -> p n t", t=4),
                    in0=banks[g][:].rearrange("p t n -> p n t"), scalar=mv[:, 0:1],
                    in1=gam[:, 512 * g : 512 * (g + 1)].rearrange("p (n t) -> p n t", t=4),
                    op0=sh_op, op1=ALU.mult)
            o = ln_pool.tile([P, S], F32, name="o")
            nc.vector.scalar_tensor_tensor(out=o[:], in0=w[:], scalar=rstd[:], in1=bet[:], op0=ALU.mult, op1=ALU.add)
            nc.sync.dma_start(out=out_view[:, i, :], in_=o[:])

        for i in range(4):
            states_tile(i)
        for g in range(2):
            for c in (1, 2, 0):
                w1_part(c, g)
        inputs_pair(0)
        cell_half(0)
        for c in range(2):
            w2_part(c)
        inputs_pair(1)
        stage1(0)
        stage1(1)
        stage2(0)
        for i in range(4, 8):
            states_tile(i)
        norm(0)
        norm(1)
        stage1(2)
        stage1(3)
        stage2(1)
        cell_half(1)
        inputs_pair(2)
        norm(2)
        norm(3)
        inputs_pair(3)
        stage1(4)
        stage1(5)
        stage2(2)
        norm(4)
        norm(5)
        stage1(6)
        stage1(7)
        stage2(3)
        norm(6)
        norm(7)
